import numpy as np
import ml_dtypes


def mxq(x, axis, fmt="e4m3"):
    dtype, down = {"e4m3": (ml_dtypes.float8_e4m3fn, 7), "e5m2": (ml_dtypes.float8_e5m2, 14)}[fmt]
    v = np.moveaxis(np.asarray(x, np.float32).astype(ml_dtypes.bfloat16).astype(np.float64), axis, -1)
    blocks = v.reshape(v.shape[:-1] + (-1, 32))
    amax = np.abs(blocks).max(-1, keepdims=True)
    byte = np.maximum(np.where(amax > 0, np.frexp(amax)[1] - 1 + 127, 0) - down, 1)
    scale = np.exp2(byte - 127.0)
    codes = (blocks / scale).astype(np.float32).astype(dtype).astype(np.float64)
    return np.moveaxis((codes * scale).reshape(v.shape), -1, axis)


WIDE = False


def mx_kscale(k):
    if not WIDE:
        return np.ones(k)
    levels = np.array([10, -10, 5, -5, 0])
    a = np.random.permutation(np.resize(levels, k // 512 * 4)).reshape(k // 512, 4)
    idx = np.arange(k)
    return np.exp2(a[idx // 512, idx % 128 // 32])


BF16 = ml_dtypes.bfloat16


def bf(x):
    return np.asarray(x, np.float32).astype(BF16)


def f64(x):
    return np.asarray(x).astype(np.float64)


E, D_COMM, D_REL, D_HET, D_HID = 16384, 1024, 512, 128, 512
D_IN = D_COMM + D_REL


def setup_inputs():
    s, t = mx_kscale(D_REL), mx_kscale(D_HID)
    spread = np.exp(0.5 * np.random.standard_normal((E, 1)))
    return {"Mij": bf(np.random.standard_normal((E, D_REL)) * s),
            "f_weights": bf(np.random.standard_normal((E, D_HET)) * np.sqrt(2.0 / D_HET) * spread),
            "W1_rel": bf(np.random.standard_normal((D_REL, D_HID)) / np.sqrt(D_IN) / s[:, None] * t),
            "node_bias": bf(np.random.standard_normal(D_HID) * np.sqrt(D_COMM / D_IN) * t),
            "W2": bf(np.random.standard_normal((D_HID, D_HET)) / np.sqrt(D_HID) / t[:, None]),
            "b2": bf(np.random.standard_normal(D_HET) * 0.1)}


def reference(Mij, f_weights, W1_rel, node_bias, W2, b2):
    h = np.maximum((mxq(f64(Mij), 1, "e4m3") @ mxq(f64(W1_rel), 0, "e4m3")) + f64(node_bias), 0.0)
    out = (mxq(h, 1, "e4m3") @ mxq(f64(W2), 0, "e4m3")) + f64(b2)
    msg = out * f64(f_weights)
    norm = np.sqrt((msg * msg).sum(axis=1, keepdims=True))
    scale = np.where(norm > 1.0, 1.0 / np.maximum(norm, 1.0), 1.0)
    return msg * scale

@@ -1,0 +1,284 @@
+from contextlib import ExitStack
+
+import concourse.mybir as mybir
+from concourse.masks import make_identity
+
+F32 = mybir.dt.float32
+BF16 = mybir.dt.bfloat16
+U32 = mybir.dt.uint32
+U8 = mybir.dt.uint8
+FP8X4 = mybir.dt.float8_e4m3fn_x4
+ACT = mybir.ActivationFunctionType
+ALU = mybir.AluOpType
+
+E, D_REL, D_HID, D_HET = 16384, 512, 512, 128
+FLOPS = 2 * E * (D_REL * D_HID + D_HID * D_HET)
+
+P = 128
+PACK = 4
+CHUNK = 512
+SUBTILES = CHUNK // P
+BLOCK = 1024
+CHUNKS_PER_BLOCK = BLOCK // CHUNK
+EDGES_PER_PARTITION = BLOCK // P
+N_CHUNKS = E // CHUNK
+N_BLOCKS = E // BLOCK
+WORDS = D_REL // 2
+
+
+def tile_filter_pa_t_kernel(tc, Mij, f_weights, W1_rel, node_bias, W2, b2, out):
+    nc = tc.nc
+    with ExitStack() as ctx:
+        consts = ctx.enter_context(tc.tile_pool(name="consts", bufs=1))
+        mij_pool = ctx.enter_context(tc.tile_pool(name="mij", bufs=3))
+        f_pool = ctx.enter_context(tc.tile_pool(name="fw", bufs=6))
+        work = ctx.enter_context(tc.tile_pool(name="work", bufs=2))
+        block_pool = ctx.enter_context(tc.tile_pool(name="blocks", bufs=3))
+        xt_psum = ctx.enter_context(tc.psum_pool(name="xt", bufs=2))
+        l1_psum = ctx.enter_context(tc.psum_pool(name="l1", bufs=4))
+        l2_psum = ctx.enter_context(tc.psum_pool(name="l2", bufs=2))
+        ctx.enter_context(tc.manual_schedule())
+
+        mij_blocks, f_blocks = {}, {}
+
+        def load_block(b):
+            rows = slice(b * BLOCK, (b + 1) * BLOCK)
+            mij_blk = mij_pool.tile([P, EDGES_PER_PARTITION * D_REL], BF16)
+            nc.sync.dma_start(out=mij_blk[:], in_=Mij[rows, :].rearrange("(p a) k -> p (a k)", p=P))
+            f_blk = f_pool.tile([P, EDGES_PER_PARTITION, D_HET], BF16)
+            nc.sync.dma_start(out=f_blk[:], in_=f_weights[rows, :].rearrange("(p a) j -> p a j", p=P))
+            mij_blocks[b] = mij_blk
+            f_blocks[b] = f_blk
+
+        w1_raw = consts.tile([P, PACK, D_HID], BF16)
+        for u in range(2):
+            nc.sync.dma_start(
+                out=w1_raw[:, 2 * u : 2 * u + 2, :],
+                in_=W1_rel[256 * u : 256 * u + 256, :].rearrange("(q e) c -> q e c", e=2),
+            )
+        load_block(0)
+        w2_raw = consts.tile([P, PACK, D_HET], BF16)
+        nc.scalar.dma_start(out=w2_raw[:], in_=W2.rearrange("(p t) j -> p t j", t=PACK))
+        bias1_bf = consts.tile([P, PACK], BF16)
+        nc.scalar.dma_start(out=bias1_bf[:], in_=node_bias.rearrange("(p t) -> p t", t=PACK))
+        b2_bf = consts.tile([P, D_HET], BF16)
+        nc.scalar.dma_start(out=b2_bf[:], in_=b2.partition_broadcast(P))
+        load_block(1)
+
+        ident = consts.tile([P, P], F32)
+        make_identity(nc, ident[:])
+
+        one = consts.tile([P, 1], F32)
+        nc.vector.memset(one[:], 1.0)
+        warm = consts.tile([P, 1], F32)
+        nc.scalar.sqrt(out=warm[:], in_=one[:])
+
+        w1_grouped = consts.tile([P, D_HID, PACK], BF16, align_bytes=64)
+        nc.vector.tensor_copy(
+            out=w1_grouped[:].rearrange("p (t q) k -> p t q k", t=PACK),
+            in_=w1_raw[:].rearrange("p k (q t) -> p t q k", t=PACK),
+        )
+        w2_grouped = consts.tile([P, D_HET, PACK], BF16, align_bytes=64)
+        nc.vector.tensor_copy(out=w2_grouped[:], in_=w2_raw[:].rearrange("p t j -> p j t"))
+        w1_codes = consts.tile([P, D_HID], U32, align_bytes=64)
+        w1_scales = consts.tile([P, D_HID], U8, align_bytes=64)
+        nc.vector.quantize_mx(
+            out=w1_codes[:].bitcast(FP8X4),
+            scales=w1_scales[:],
+            in_=w1_grouped[:].rearrange("p n k -> p (n k)"),
+        )
+        w2_codes = consts.tile([P, D_HET], U32, align_bytes=64)
+        w2_scales = consts.tile([P, D_HET], U8, align_bytes=64)
+        nc.vector.quantize_mx(
+            out=w2_codes[:].bitcast(FP8X4),
+            scales=w2_scales[:],
+            in_=w2_grouped[:].rearrange("p j t -> p (j t)"),
+        )
+        bias1 = consts.tile([P, PACK], F32)
+        nc.vector.tensor_copy(out=bias1[:], in_=bias1_bf[:])
+        b2_rows = consts.tile([P, D_HET], F32)
+        nc.vector.tensor_copy(out=b2_rows[:], in_=b2_bf[:])
+
+        xt_banks, mij_grouped_of, mij_mx, h_banks, h_rows_of, h_grouped_of, h_mx = {}, {}, {}, {}, {}, {}, {}
+        out_bank_of, msg_blocks, ss_blocks, clamped_of, norm_of = {}, {}, {}, {}, {}
+
+        def transpose_mij(c):
+            words = mij_blocks[c // CHUNKS_PER_BLOCK][:].bitcast(F32)
+            first = (c % CHUNKS_PER_BLOCK) * SUBTILES
+            banks = []
+            for half in range(2):
+                xt = xt_psum.tile([P, 2, 2, P], F32)
+                for a in range(2):
+                    for u in range(2):
+                        col = (first + 2 * half + a) * WORDS + P * u
+                        nc.tensor.transpose(out=xt[:, a, u, :], in_=words[:, col : col + P], identity=ident[:])
+                banks.append(xt)
+            xt_banks[c] = banks
+
+        def gather_mij(c):
+            mij_grouped = work.tile([P, CHUNK * PACK], BF16, align_bytes=64)
+            as_words = mij_grouped[:].bitcast(F32)
+            for half in range(2):
+                nc.scalar.copy(
+                    out=as_words[:, half * CHUNK : (half + 1) * CHUNK].rearrange("p (a j u) -> p a j u", a=2, u=2),
+                    in_=xt_banks[c][half][:].rearrange("p a u j -> p a j u"),
+                )
+            mij_grouped_of[c] = mij_grouped
+
+        def quantise_mij(c):
+            mij_codes = work.tile([P, CHUNK], U32, align_bytes=64)
+            mij_scales = work.tile([P, CHUNK], U8, align_bytes=64)
+            nc.vector.quantize_mx(out=mij_codes[:].bitcast(FP8X4), scales=mij_scales[:], in_=mij_grouped_of[c][:])
+            mij_mx[c] = (mij_codes, mij_scales)
+
+        def layer1(c):
+            mij_codes, mij_scales = mij_mx[c]
+            banks = []
+            for t in range(PACK):
+                units = slice(t * P, (t + 1) * P)
+                acc = l1_psum.tile([P, CHUNK], F32)
+                nc.tensor.matmul_mx(
+                    out=acc[:],
+                    lhsT=w1_codes[:, units].bitcast(FP8X4),
+                    lhsT_scale=w1_scales[:, units],
+                    rhs=mij_codes[:].bitcast(FP8X4),
+                    rhs_scale=mij_scales[:],
+                    start=True,
+                    stop=True,
+                )
+                banks.append(acc)
+            h_banks[c] = banks
+
+        def bias_relu(c):
+            h_rows = work.tile([P, PACK, CHUNK], BF16)
+            for t in range(PACK):
+                nc.scalar.activation(
+                    out=h_rows[:, t, :], in_=h_banks[c][t][:], func=ACT.Relu, bias=bias1[:, t : t + 1], scale=1.0
+                )
+            h_rows_of[c] = h_rows
+
+        def regroup_h(c):
+            h_grouped = work.tile([P, CHUNK, PACK], BF16, align_bytes=64)
+            nc.vector.tensor_copy(
+                out=h_grouped[:].rearrange("p (c i) t -> p c t i", i=4),
+                in_=h_rows_of[c][:].rearrange("p t (c i) -> p c t i", i=4),
+            )
+            h_grouped_of[c] = h_grouped
+
+        def quantise_h(c):
+            h_codes = work.tile([P, CHUNK], U32, align_bytes=64)
+            h_scales = work.tile([P, CHUNK], U8, align_bytes=64)
+            nc.vector.quantize_mx(
+                out=h_codes[:].bitcast(FP8X4), scales=h_scales[:], in_=h_grouped_of[c][:].rearrange("p e t -> p (e t)")
+            )
+            h_mx[c] = (h_codes, h_scales)
+
+        def layer2(c):
+            h_codes, h_scales = h_mx[c]
+            out_bank = l2_psum.tile([P, SUBTILES, D_HET], F32)
+            for a in range(SUBTILES):
+                edges = slice(a * P, (a + 1) * P)
+                nc.tensor.matmul_mx(
+                    out=out_bank[:, a, :],
+                    lhsT=h_codes[:, edges].bitcast(FP8X4),
+                    lhsT_scale=h_scales[:, edges],
+                    rhs=w2_codes[:].bitcast(FP8X4),
+                    rhs_scale=w2_scales[:],
+                    start=True,
+                    stop=True,
+                )
+            out_bank_of[c] = out_bank
+
+        def message(c):
+            b = c // CHUNKS_PER_BLOCK
+            if c % CHUNKS_PER_BLOCK == 0:
+                msg_blk = block_pool.tile([P, EDGES_PER_PARTITION, D_HET], F32)
+                msg_blocks[b] = msg_blk
+            first = (c % CHUNKS_PER_BLOCK) * SUBTILES
+            biased = work.tile([P, SUBTILES, D_HET], F32)
+            nc.vector.tensor_tensor(
+                out=biased[:],
+                in0=out_bank_of[c][:],
+                in1=b2_rows[:].unsqueeze(1).to_broadcast([P, SUBTILES, D_HET]),
+                op=ALU.add,
+            )
+            nc.vector.tensor_tensor(
+                out=msg_blocks[b][:, first : first + SUBTILES, :],
+                in0=biased[:],
+                in1=f_blocks[b][:, first : first + SUBTILES, :],
+                op=ALU.mult,
+            )
+
+        def sum_squares(c):
+            b = c // CHUNKS_PER_BLOCK
+            if c % CHUNKS_PER_BLOCK == 0:
+                ss_blk = block_pool.tile([P, EDGES_PER_PARTITION], F32)
+                ss_blocks[b] = ss_blk
+            first = (c % CHUNKS_PER_BLOCK) * SUBTILES
+            squares = work.tile([P, SUBTILES, D_HET], BF16)
+            for a in range(SUBTILES):
+                nc.scalar.activation(
+                    out=squares[:, a, :],
+                    in_=msg_blocks[b][:, first + a, :],
+                    func=ACT.Square,
+                    accum_out=ss_blocks[b][:, first + a : first + a + 1],
+                )
+
+        def clamp_sum(b):
+            clamped = block_pool.tile([P, EDGES_PER_PARTITION], F32)
+            nc.vector.tensor_scalar_max(out=clamped[:], in0=ss_blocks[b][:], scalar1=1.0)
+            clamped_of[b] = clamped
+
+        def root(b):
+            norm = block_pool.tile([P, EDGES_PER_PARTITION], F32)
+            nc.scalar.sqrt(out=norm[:], in_=clamped_of[b][:])
+            norm_of[b] = norm
+
+        def scale_and_store(b):
+            factor = block_pool.tile([P, EDGES_PER_PARTITION], F32)
+            nc.vector.reciprocal(out=factor[:], in_=norm_of[b][:])
+            result = block_pool.tile([P, EDGES_PER_PARTITION, D_HET], F32)
+            nc.vector.tensor_tensor(
+                out=result[:],
+                in0=msg_blocks[b][:],
+                in1=factor[:].unsqueeze(2).to_broadcast([P, EDGES_PER_PARTITION, D_HET]),
+                op=ALU.mult,
+            )
+            rows = slice(b * BLOCK, (b + 1) * BLOCK)
+            nc.sync.dma_start(out=out[rows, :].rearrange("(p a) j -> p a j", p=P), in_=result[:])
+
+        def chunk(c):
+            return 0 <= c < N_CHUNKS
+
+        def closes_block(c):
+            return chunk(c) and c % CHUNKS_PER_BLOCK == CHUNKS_PER_BLOCK - 1
+
+        transpose_mij(0)
+        for w in range(N_CHUNKS + 8):
+            if closes_block(w - 6):
+                clamp_sum((w - 6) // CHUNKS_PER_BLOCK)
+            if chunk(w):
+                gather_mij(w)
+            if chunk(w - 1):
+                quantise_mij(w - 1)
+            if chunk(w + 1):
+                transpose_mij(w + 1)
+            if w % CHUNKS_PER_BLOCK == 0 and w // CHUNKS_PER_BLOCK + 2 < N_BLOCKS:
+                load_block(w // CHUNKS_PER_BLOCK + 2)
+            if chunk(w - 2):
+                bias_relu(w - 2)
+            if chunk(w - 1):
+                layer1(w - 1)
+            if chunk(w - 3):
+                regroup_h(w - 3)
+            if chunk(w - 4):
+                message(w - 4)
+            if chunk(w - 3):
+                quantise_h(w - 3)
+                layer2(w - 3)
+            if chunk(w - 5):
+                sum_squares(w - 5)
+            if closes_block(w - 6):
+                root((w - 6) // CHUNKS_PER_BLOCK)
+            if closes_block(w - 7):
+                scale_and_store((w - 7) // CHUNKS_PER_BLOCK)

@@ -30,40 +30,48 @@ def tile_filter_pa_t_kernel(tc, Mij, f_weights, W1_rel, node_bias, W2, b2, out):
     nc = tc.nc
     with ExitStack() as ctx:
         consts = ctx.enter_context(tc.tile_pool(name="consts", bufs=1))
-        mij_pool = ctx.enter_context(tc.tile_pool(name="mij", bufs=3))
-        f_pool = ctx.enter_context(tc.tile_pool(name="fw", bufs=6))
+        mij_pool = ctx.enter_context(tc.tile_pool(name="mij", bufs=4))
+        f_pool = ctx.enter_context(tc.tile_pool(name="fw", bufs=5))
         work = ctx.enter_context(tc.tile_pool(name="work", bufs=2))
         block_pool = ctx.enter_context(tc.tile_pool(name="blocks", bufs=3))
         xt_psum = ctx.enter_context(tc.psum_pool(name="xt", bufs=2))
         l1_psum = ctx.enter_context(tc.psum_pool(name="l1", bufs=4))
         l2_psum = ctx.enter_context(tc.psum_pool(name="l2", bufs=2))
-        ctx.enter_context(tc.manual_schedule())
 
-        mij_blocks, f_blocks = {}, {}
+        mij_rows_of, f_blocks = {}, {}
 
-        def load_block(b):
-            rows = slice(b * BLOCK, (b + 1) * BLOCK)
-            mij_blk = mij_pool.tile([P, EDGES_PER_PARTITION * D_REL], BF16)
-            nc.sync.dma_start(out=mij_blk[:], in_=Mij[rows, :].rearrange("(p a) k -> p (a k)", p=P))
-            f_blk = f_pool.tile([P, EDGES_PER_PARTITION, D_HET], BF16)
-            nc.sync.dma_start(out=f_blk[:], in_=f_weights[rows, :].rearrange("(p a) j -> p a j", p=P))
-            mij_blocks[b] = mij_blk
-            f_blocks[b] = f_blk
+        def block_rows(dram, b):
+            return dram[b * BLOCK : (b + 1) * BLOCK, :].rearrange("(p a) k -> p a k", p=P)
 
+        def own_edges(c):
+            first = (c % CHUNKS_PER_BLOCK) * SUBTILES
+            return slice(first, first + SUBTILES)
+
+        def load_chunk(c):
+            b = c // CHUNKS_PER_BLOCK
+            mij_rows = mij_pool.tile([P, SUBTILES, D_REL], BF16)
+            nc.sync.dma_start(out=mij_rows[:], in_=block_rows(Mij, b)[:, own_edges(c), :])
+            mij_rows_of[c] = mij_rows
+            if c % CHUNKS_PER_BLOCK == 0:
+                f_blk = f_pool.tile([P, EDGES_PER_PARTITION, D_HET], BF16)
+                nc.sync.dma_start(out=f_blk[:], in_=block_rows(f_weights, b))
+                f_blocks[b] = f_blk
+
+        load_chunk(0)
         w1_raw = consts.tile([P, PACK, D_HID], BF16)
         for u in range(2):
             nc.sync.dma_start(
                 out=w1_raw[:, 2 * u : 2 * u + 2, :],
                 in_=W1_rel[256 * u : 256 * u + 256, :].rearrange("(q e) c -> q e c", e=2),
             )
-        load_block(0)
+        load_chunk(1)
         w2_raw = consts.tile([P, PACK, D_HET], BF16)
         nc.scalar.dma_start(out=w2_raw[:], in_=W2.rearrange("(p t) j -> p t j", t=PACK))
         bias1_bf = consts.tile([P, PACK], BF16)
         nc.scalar.dma_start(out=bias1_bf[:], in_=node_bias.rearrange("(p t) -> p t", t=PACK))
         b2_bf = consts.tile([P, D_HET], BF16)
         nc.scalar.dma_start(out=b2_bf[:], in_=b2.partition_broadcast(P))
-        load_block(1)
+        load_chunk(2)
 
         ident = consts.tile([P, P], F32)
         make_identity(nc, ident[:])
@@ -100,17 +108,16 @@ def tile_filter_pa_t_kernel(tc, Mij, f_weights, W1_rel, node_bias, W2, b2, out):
         nc.vector.tensor_copy(out=b2_rows[:], in_=b2_bf[:])
 
         xt_banks, mij_grouped_of, mij_mx, h_banks, h_rows_of, h_grouped_of, h_mx = {}, {}, {}, {}, {}, {}, {}
-        out_bank_of, msg_blocks, ss_blocks, clamped_of, norm_of = {}, {}, {}, {}, {}
+        out_bank_of, msg_blocks, ss_blocks, clamped_of, norm_of, factor_of = {}, {}, {}, {}, {}, {}
 
         def transpose_mij(c):
-            words = mij_blocks[c // CHUNKS_PER_BLOCK][:].bitcast(F32)
-            first = (c % CHUNKS_PER_BLOCK) * SUBTILES
+            words = mij_rows_of[c][:].rearrange("p a k -> p (a k)").bitcast(F32)
             banks = []
             for half in range(2):
                 xt = xt_psum.tile([P, 2, 2, P], F32)
                 for a in range(2):
                     for u in range(2):
-                        col = (first + 2 * half + a) * WORDS + P * u
+                        col = (2 * half + a) * WORDS + P * u
                         nc.tensor.transpose(out=xt[:, a, u, :], in_=words[:, col : col + P], identity=ident[:])
                 banks.append(xt)
             xt_banks[c] = banks
@@ -194,7 +201,6 @@ def tile_filter_pa_t_kernel(tc, Mij, f_weights, W1_rel, node_bias, W2, b2, out):
             if c % CHUNKS_PER_BLOCK == 0:
                 msg_blk = block_pool.tile([P, EDGES_PER_PARTITION, D_HET], F32)
                 msg_blocks[b] = msg_blk
-            first = (c % CHUNKS_PER_BLOCK) * SUBTILES
             biased = work.tile([P, SUBTILES, D_HET], F32)
             nc.vector.tensor_tensor(
                 out=biased[:],
@@ -203,9 +209,9 @@ def tile_filter_pa_t_kernel(tc, Mij, f_weights, W1_rel, node_bias, W2, b2, out):
                 op=ALU.add,
             )
             nc.vector.tensor_tensor(
-                out=msg_blocks[b][:, first : first + SUBTILES, :],
+                out=msg_blocks[b][:, own_edges(c), :],
                 in0=biased[:],
-                in1=f_blocks[b][:, first : first + SUBTILES, :],
+                in1=f_blocks[b][:, own_edges(c), :],
                 op=ALU.mult,
             )
 
@@ -234,51 +240,53 @@ def tile_filter_pa_t_kernel(tc, Mij, f_weights, W1_rel, node_bias, W2, b2, out):
             nc.scalar.sqrt(out=norm[:], in_=clamped_of[b][:])
             norm_of[b] = norm
 
-        def scale_and_store(b):
+        def invert(b):
             factor = block_pool.tile([P, EDGES_PER_PARTITION], F32)
             nc.vector.reciprocal(out=factor[:], in_=norm_of[b][:])
-            result = block_pool.tile([P, EDGES_PER_PARTITION, D_HET], F32)
+            factor_of[b] = factor
+
+        def scale_and_store(c):
+            b = c // CHUNKS_PER_BLOCK
+            result = work.tile([P, SUBTILES, D_HET], F32, bufs=3)
             nc.vector.tensor_tensor(
                 out=result[:],
-                in0=msg_blocks[b][:],
-                in1=factor[:].unsqueeze(2).to_broadcast([P, EDGES_PER_PARTITION, D_HET]),
+                in0=msg_blocks[b][:, own_edges(c), :],
+                in1=factor_of[b][:, own_edges(c)].unsqueeze(2).to_broadcast([P, SUBTILES, D_HET]),
                 op=ALU.mult,
             )
-            rows = slice(b * BLOCK, (b + 1) * BLOCK)
-            nc.sync.dma_start(out=out[rows, :].rearrange("(p a) j -> p a j", p=P), in_=result[:])
+            nc.sync.dma_start(out=block_rows(out, b)[:, own_edges(c), :], in_=result[:])
 
         def chunk(c):
             return 0 <= c < N_CHUNKS
 
-        def closes_block(c):
-            return chunk(c) and c % CHUNKS_PER_BLOCK == CHUNKS_PER_BLOCK - 1
-
         transpose_mij(0)
-        for w in range(N_CHUNKS + 8):
-            if closes_block(w - 6):
-                clamp_sum((w - 6) // CHUNKS_PER_BLOCK)
+        for w in range(N_CHUNKS + 6):
+            new_factors = chunk(w - 5) and (w - 5) % CHUNKS_PER_BLOCK == 0
+            if new_factors:
+                clamp_sum((w - 5) // CHUNKS_PER_BLOCK)
             if chunk(w):
                 gather_mij(w)
-            if chunk(w - 1):
-                quantise_mij(w - 1)
+            if new_factors:
+                root((w - 5) // CHUNKS_PER_BLOCK)
             if chunk(w + 1):
                 transpose_mij(w + 1)
-            if w % CHUNKS_PER_BLOCK == 0 and w // CHUNKS_PER_BLOCK + 2 < N_BLOCKS:
-                load_block(w // CHUNKS_PER_BLOCK + 2)
+            if chunk(w + 3):
+                load_chunk(w + 3)
             if chunk(w - 2):
-                bias_relu(w - 2)
+                regroup_h(w - 2)
+            if chunk(w - 3):
+                message(w - 3)
             if chunk(w - 1):
-                layer1(w - 1)
+                bias_relu(w - 1)
+            if chunk(w):
+                quantise_mij(w)
+                layer1(w)
+            if chunk(w - 2):
+                quantise_h(w - 2)
+                layer2(w - 2)
             if chunk(w - 3):
-                regroup_h(w - 3)
-            if chunk(w - 4):
-                message(w - 4)
-            if chunk(w - 3):
-                quantise_h(w - 3)
-                layer2(w - 3)
+                sum_squares(w - 3)
+            if new_factors:
+                invert((w - 5) // CHUNKS_PER_BLOCK)
             if chunk(w - 5):
-                sum_squares(w - 5)
-            if closes_block(w - 6):
-                root((w - 6) // CHUNKS_PER_BLOCK)
-            if closes_block(w - 7):
-                scale_and_store((w - 7) // CHUNKS_PER_BLOCK)
+                scale_and_store(w - 5)

@@ -159,9 +159,19 @@ def tile_filter_pa_t_kernel(tc, Mij, f_weights, W1_rel, node_bias, W2, b2, out):
         def bias_relu(c):
             h_rows = work.tile([P, PACK, CHUNK], BF16)
             for t in range(PACK):
-                nc.scalar.activation(
-                    out=h_rows[:, t, :], in_=h_banks[c][t][:], func=ACT.Relu, bias=bias1[:, t : t + 1], scale=1.0
-                )
+                if t == PACK - 1 and c % 2 == 1:
+                    nc.vector.tensor_scalar(
+                        out=h_rows[:, t, :],
+                        in0=h_banks[c][t][:],
+                        scalar1=bias1[:, t : t + 1],
+                        scalar2=0.0,
+                        op0=ALU.add,
+                        op1=ALU.max,
+                    )
+                else:
+                    nc.scalar.activation(
+                        out=h_rows[:, t, :], in_=h_banks[c][t][:], func=ACT.Relu, bias=bias1[:, t : t + 1], scale=1.0
+                    )
             h_rows_of[c] = h_rows
 
         def regroup_h(c):

@@ -24,6 +24,9 @@ EDGES_PER_PARTITION = BLOCK // P
 N_CHUNKS = E // CHUNK
 N_BLOCKS = E // BLOCK
 WORDS = D_REL // 2
+HEAD_CHUNKS = 3
+TAIL_CHUNKS = 4
+SCALAR_SCALES_EVERY = 4
 
 
 def tile_filter_pa_t_kernel(tc, Mij, f_weights, W1_rel, node_bias, W2, b2, out):
@@ -108,7 +111,7 @@ def tile_filter_pa_t_kernel(tc, Mij, f_weights, W1_rel, node_bias, W2, b2, out):
         nc.vector.tensor_copy(out=b2_rows[:], in_=b2_bf[:])
 
         xt_banks, mij_grouped_of, mij_mx, h_banks, h_rows_of, h_grouped_of, h_mx = {}, {}, {}, {}, {}, {}, {}
-        out_bank_of, msg_blocks, ss_blocks, clamped_of, norm_of, factor_of = {}, {}, {}, {}, {}, {}
+        out_bank_of, msg_blocks, ss_blocks, clamped_of, norm_of, factor_of, biased_of = {}, {}, {}, {}, {}, {}, {}
 
         def transpose_mij(c):
             words = mij_rows_of[c][:].rearrange("p a k -> p (a k)").bitcast(F32)
@@ -126,10 +129,12 @@ def tile_filter_pa_t_kernel(tc, Mij, f_weights, W1_rel, node_bias, W2, b2, out):
             mij_grouped = work.tile([P, CHUNK * PACK], BF16, align_bytes=64)
             as_words = mij_grouped[:].bitcast(F32)
             for half in range(2):
-                nc.scalar.copy(
-                    out=as_words[:, half * CHUNK : (half + 1) * CHUNK].rearrange("p (a j u) -> p a j u", a=2, u=2),
-                    in_=xt_banks[c][half][:].rearrange("p a u j -> p a j u"),
-                )
+                side_by_side = as_words[:, half * CHUNK : (half + 1) * CHUNK].rearrange("p (a j u) -> p a j u", a=2, u=2)
+                planes = xt_banks[c][half][:].rearrange("p a u j -> p a j u")
+                if c < HEAD_CHUNKS:
+                    nc.vector.tensor_copy(out=side_by_side, in_=planes)
+                else:
+                    nc.scalar.copy(out=side_by_side, in_=planes)
             mij_grouped_of[c] = mij_grouped
 
         def quantise_mij(c):
@@ -159,19 +164,9 @@ def tile_filter_pa_t_kernel(tc, Mij, f_weights, W1_rel, node_bias, W2, b2, out):
         def bias_relu(c):
             h_rows = work.tile([P, PACK, CHUNK], BF16)
             for t in range(PACK):
-                if t == PACK - 1 and c % 2 == 1:
-                    nc.vector.tensor_scalar(
-                        out=h_rows[:, t, :],
-                        in0=h_banks[c][t][:],
-                        scalar1=bias1[:, t : t + 1],
-                        scalar2=0.0,
-                        op0=ALU.add,
-                        op1=ALU.max,
-                    )
-                else:
-                    nc.scalar.activation(
-                        out=h_rows[:, t, :], in_=h_banks[c][t][:], func=ACT.Relu, bias=bias1[:, t : t + 1], scale=1.0
-                    )
+                nc.scalar.activation(
+                    out=h_rows[:, t, :], in_=h_banks[c][t][:], func=ACT.Relu, bias=bias1[:, t : t + 1], scale=1.0
+                )
             h_rows_of[c] = h_rows
 
         def regroup_h(c):
@@ -206,11 +201,7 @@ def tile_filter_pa_t_kernel(tc, Mij, f_weights, W1_rel, node_bias, W2, b2, out):
                 )
             out_bank_of[c] = out_bank
 
-        def message(c):
-            b = c // CHUNKS_PER_BLOCK
-            if c % CHUNKS_PER_BLOCK == 0:
-                msg_blk = block_pool.tile([P, EDGES_PER_PARTITION, D_HET], F32)
-                msg_blocks[b] = msg_blk
+        def add_b2(c):
             biased = work.tile([P, SUBTILES, D_HET], F32)
             nc.vector.tensor_tensor(
                 out=biased[:],
@@ -218,9 +209,16 @@ def tile_filter_pa_t_kernel(tc, Mij, f_weights, W1_rel, node_bias, W2, b2, out):
                 in1=b2_rows[:].unsqueeze(1).to_broadcast([P, SUBTILES, D_HET]),
                 op=ALU.add,
             )
+            biased_of[c] = biased
+
+        def message(c):
+            b = c // CHUNKS_PER_BLOCK
+            if c % CHUNKS_PER_BLOCK == 0:
+                msg_blk = block_pool.tile([P, EDGES_PER_PARTITION, D_HET], F32)
+                msg_blocks[b] = msg_blk
             nc.vector.tensor_tensor(
                 out=msg_blocks[b][:, own_edges(c), :],
-                in0=biased[:],
+                in0=biased_of[c][:],
                 in1=f_blocks[b][:, own_edges(c), :],
                 op=ALU.mult,
             )
@@ -258,19 +256,29 @@ def tile_filter_pa_t_kernel(tc, Mij, f_weights, W1_rel, node_bias, W2, b2, out):
         def scale_and_store(c):
             b = c // CHUNKS_PER_BLOCK
             result = work.tile([P, SUBTILES, D_HET], F32, bufs=3)
-            nc.vector.tensor_tensor(
-                out=result[:],
-                in0=msg_blocks[b][:, own_edges(c), :],
-                in1=factor_of[b][:, own_edges(c)].unsqueeze(2).to_broadcast([P, SUBTILES, D_HET]),
-                op=ALU.mult,
-            )
+            if c < N_CHUNKS - TAIL_CHUNKS and c % SCALAR_SCALES_EVERY != SCALAR_SCALES_EVERY - 1:
+                nc.vector.tensor_tensor(
+                    out=result[:],
+                    in0=msg_blocks[b][:, own_edges(c), :],
+                    in1=factor_of[b][:, own_edges(c)].unsqueeze(2).to_broadcast([P, SUBTILES, D_HET]),
+                    op=ALU.mult,
+                )
+            else:
+                first = (c % CHUNKS_PER_BLOCK) * SUBTILES
+                for a in range(SUBTILES):
+                    nc.scalar.activation(
+                        out=result[:, a, :],
+                        in_=msg_blocks[b][:, first + a, :],
+                        func=ACT.Copy,
+                        scale=factor_of[b][:, first + a : first + a + 1],
+                    )
             nc.sync.dma_start(out=block_rows(out, b)[:, own_edges(c), :], in_=result[:])
 
         def chunk(c):
             return 0 <= c < N_CHUNKS
 
         transpose_mij(0)
-        for w in range(N_CHUNKS + 6):
+        for w in range(N_CHUNKS + 7):
             new_factors = chunk(w - 5) and (w - 5) % CHUNKS_PER_BLOCK == 0
             if new_factors:
                 clamp_sum((w - 5) // CHUNKS_PER_BLOCK)
@@ -285,18 +293,20 @@ def tile_filter_pa_t_kernel(tc, Mij, f_weights, W1_rel, node_bias, W2, b2, out):
             if chunk(w - 2):
                 regroup_h(w - 2)
             if chunk(w - 3):
-                message(w - 3)
+                add_b2(w - 3)
             if chunk(w - 1):
                 bias_relu(w - 1)
             if chunk(w):
                 quantise_mij(w)
                 layer1(w)
+            if chunk(w - 3):
+                message(w - 3)
             if chunk(w - 2):
                 quantise_h(w - 2)
                 layer2(w - 2)
             if chunk(w - 3):
                 sum_squares(w - 3)
+            if chunk(w - 6):
+                scale_and_store(w - 6)
             if new_factors:
                 invert((w - 5) // CHUNKS_PER_BLOCK)
-            if chunk(w - 5):
-                scale_and_store(w - 5)

from contextlib import ExitStack

import concourse.mybir as mybir
from concourse.masks import make_identity

F32 = mybir.dt.float32
BF16 = mybir.dt.bfloat16
U32 = mybir.dt.uint32
U8 = mybir.dt.uint8
FP8X4 = mybir.dt.float8_e4m3fn_x4
ACT = mybir.ActivationFunctionType
ALU = mybir.AluOpType

E, D_REL, D_HID, D_HET = 16384, 512, 512, 128
FLOPS = 2 * E * (D_REL * D_HID + D_HID * D_HET)

P = 128
PACK = 4
CHUNK = 512
SUBTILES = CHUNK // P
BLOCK = 1024
CHUNKS_PER_BLOCK = BLOCK // CHUNK
EDGES_PER_PARTITION = BLOCK // P
N_CHUNKS = E // CHUNK
N_BLOCKS = E // BLOCK
WORDS = D_REL // 2
HEAD_CHUNKS = 3
TAIL_CHUNKS = 4
SCALAR_SCALES_EVERY = 4


def tile_filter_pa_t_kernel(tc, Mij, f_weights, W1_rel, node_bias, W2, b2, out):
    nc = tc.nc
    with ExitStack() as ctx:
        consts = ctx.enter_context(tc.tile_pool(name="consts", bufs=1))
        mij_pool = ctx.enter_context(tc.tile_pool(name="mij", bufs=4))
        f_pool = ctx.enter_context(tc.tile_pool(name="fw", bufs=5))
        work = ctx.enter_context(tc.tile_pool(name="work", bufs=2))
        block_pool = ctx.enter_context(tc.tile_pool(name="blocks", bufs=3))
        xt_psum = ctx.enter_context(tc.psum_pool(name="xt", bufs=2))
        l1_psum = ctx.enter_context(tc.psum_pool(name="l1", bufs=4))
        l2_psum = ctx.enter_context(tc.psum_pool(name="l2", bufs=2))

        mij_rows_of, f_blocks = {}, {}

        def block_rows(dram, b):
            return dram[b * BLOCK : (b + 1) * BLOCK, :].rearrange("(p a) k -> p a k", p=P)

        def own_edges(c):
            first = (c % CHUNKS_PER_BLOCK) * SUBTILES
            return slice(first, first + SUBTILES)

        def load_chunk(c):
            b = c // CHUNKS_PER_BLOCK
            mij_rows = mij_pool.tile([P, SUBTILES, D_REL], BF16)
            nc.sync.dma_start(out=mij_rows[:], in_=block_rows(Mij, b)[:, own_edges(c), :])
            mij_rows_of[c] = mij_rows
            if c % CHUNKS_PER_BLOCK == 0:
                f_blk = f_pool.tile([P, EDGES_PER_PARTITION, D_HET], BF16)
                nc.sync.dma_start(out=f_blk[:], in_=block_rows(f_weights, b))
                f_blocks[b] = f_blk

        load_chunk(0)
        w1_raw = consts.tile([P, PACK, D_HID], BF16)
        for u in range(2):
            nc.sync.dma_start(
                out=w1_raw[:, 2 * u : 2 * u + 2, :],
                in_=W1_rel[256 * u : 256 * u + 256, :].rearrange("(q e) c -> q e c", e=2),
            )
        load_chunk(1)
        w2_raw = consts.tile([P, PACK, D_HET], BF16)
        nc.scalar.dma_start(out=w2_raw[:], in_=W2.rearrange("(p t) j -> p t j", t=PACK))
        bias1_bf = consts.tile([P, PACK], BF16)
        nc.scalar.dma_start(out=bias1_bf[:], in_=node_bias.rearrange("(p t) -> p t", t=PACK))
        b2_bf = consts.tile([P, D_HET], BF16)
        nc.scalar.dma_start(out=b2_bf[:], in_=b2.partition_broadcast(P))
        load_chunk(2)

        ident = consts.tile([P, P], F32)
        make_identity(nc, ident[:])

        one = consts.tile([P, 1], F32)
        nc.vector.memset(one[:], 1.0)
        warm = consts.tile([P, 1], F32)
        nc.scalar.sqrt(out=warm[:], in_=one[:])

        w1_grouped = consts.tile([P, D_HID, PACK], BF16, align_bytes=64)
        nc.vector.tensor_copy(
            out=w1_grouped[:].rearrange("p (t q) k -> p t q k", t=PACK),
            in_=w1_raw[:].rearrange("p k (q t) -> p t q k", t=PACK),
        )
        w2_grouped = consts.tile([P, D_HET, PACK], BF16, align_bytes=64)
        nc.vector.tensor_copy(out=w2_grouped[:], in_=w2_raw[:].rearrange("p t j -> p j t"))
        w1_codes = consts.tile([P, D_HID], U32, align_bytes=64)
        w1_scales = consts.tile([P, D_HID], U8, align_bytes=64)
        nc.vector.quantize_mx(
            out=w1_codes[:].bitcast(FP8X4),
            scales=w1_scales[:],
            in_=w1_grouped[:].rearrange("p n k -> p (n k)"),
        )
        w2_codes = consts.tile([P, D_HET], U32, align_bytes=64)
        w2_scales = consts.tile([P, D_HET], U8, align_bytes=64)
        nc.vector.quantize_mx(
            out=w2_codes[:].bitcast(FP8X4),
            scales=w2_scales[:],
            in_=w2_grouped[:].rearrange("p j t -> p (j t)"),
        )
        bias1 = consts.tile([P, PACK], F32)
        nc.vector.tensor_copy(out=bias1[:], in_=bias1_bf[:])
        b2_rows = consts.tile([P, D_HET], F32)
        nc.vector.tensor_copy(out=b2_rows[:], in_=b2_bf[:])

        xt_banks, mij_grouped_of, mij_mx, h_banks, h_rows_of, h_grouped_of, h_mx = {}, {}, {}, {}, {}, {}, {}
        out_bank_of, msg_blocks, ss_blocks, clamped_of, norm_of, factor_of, biased_of = {}, {}, {}, {}, {}, {}, {}

        def transpose_mij(c):
            words = mij_rows_of[c][:].rearrange("p a k -> p (a k)").bitcast(F32)
            banks = []
            for half in range(2):
                xt = xt_psum.tile([P, 2, 2, P], F32)
                for a in range(2):
                    for u in range(2):
                        col = (2 * half + a) * WORDS + P * u
                        nc.tensor.transpose(out=xt[:, a, u, :], in_=words[:, col : col + P], identity=ident[:])
                banks.append(xt)
            xt_banks[c] = banks

        def gather_mij(c):
            mij_grouped = work.tile([P, CHUNK * PACK], BF16, align_bytes=64)
            as_words = mij_grouped[:].bitcast(F32)
            for half in range(2):
                side_by_side = as_words[:, half * CHUNK : (half + 1) * CHUNK].rearrange("p (a j u) -> p a j u", a=2, u=2)
                planes = xt_banks[c][half][:].rearrange("p a u j -> p a j u")
                if c < HEAD_CHUNKS:
                    nc.vector.tensor_copy(out=side_by_side, in_=planes)
                else:
                    nc.scalar.copy(out=side_by_side, in_=planes)
            mij_grouped_of[c] = mij_grouped

        def quantise_mij(c):
            mij_codes = work.tile([P, CHUNK], U32, align_bytes=64)
            mij_scales = work.tile([P, CHUNK], U8, align_bytes=64)
            nc.vector.quantize_mx(out=mij_codes[:].bitcast(FP8X4), scales=mij_scales[:], in_=mij_grouped_of[c][:])
            mij_mx[c] = (mij_codes, mij_scales)

        def layer1(c):
            mij_codes, mij_scales = mij_mx[c]
            banks = []
            for t in range(PACK):
                units = slice(t * P, (t + 1) * P)
                acc = l1_psum.tile([P, CHUNK], F32)
                nc.tensor.matmul_mx(
                    out=acc[:],
                    lhsT=w1_codes[:, units].bitcast(FP8X4),
                    lhsT_scale=w1_scales[:, units],
                    rhs=mij_codes[:].bitcast(FP8X4),
                    rhs_scale=mij_scales[:],
                    start=True,
                    stop=True,
                )
                banks.append(acc)
            h_banks[c] = banks

        def bias_relu(c):
            h_rows = work.tile([P, PACK, CHUNK], BF16)
            for t in range(PACK):
                nc.scalar.activation(
                    out=h_rows[:, t, :], in_=h_banks[c][t][:], func=ACT.Relu, bias=bias1[:, t : t + 1], scale=1.0
                )
            h_rows_of[c] = h_rows

        def regroup_h(c):
            h_grouped = work.tile([P, CHUNK, PACK], BF16, align_bytes=64)
            nc.vector.tensor_copy(
                out=h_grouped[:].rearrange("p (c i) t -> p c t i", i=4),
                in_=h_rows_of[c][:].rearrange("p t (c i) -> p c t i", i=4),
            )
            h_grouped_of[c] = h_grouped

        def quantise_h(c):
            h_codes = work.tile([P, CHUNK], U32, align_bytes=64)
            h_scales = work.tile([P, CHUNK], U8, align_bytes=64)
            nc.vector.quantize_mx(
                out=h_codes[:].bitcast(FP8X4), scales=h_scales[:], in_=h_grouped_of[c][:].rearrange("p e t -> p (e t)")
            )
            h_mx[c] = (h_codes, h_scales)

        def layer2(c):
            h_codes, h_scales = h_mx[c]
            out_bank = l2_psum.tile([P, SUBTILES, D_HET], F32)
            for a in range(SUBTILES):
                edges = slice(a * P, (a + 1) * P)
                nc.tensor.matmul_mx(
                    out=out_bank[:, a, :],
                    lhsT=h_codes[:, edges].bitcast(FP8X4),
                    lhsT_scale=h_scales[:, edges],
                    rhs=w2_codes[:].bitcast(FP8X4),
                    rhs_scale=w2_scales[:],
                    start=True,
                    stop=True,
                )
            out_bank_of[c] = out_bank

        def add_b2(c):
            biased = work.tile([P, SUBTILES, D_HET], F32)
            nc.vector.tensor_tensor(
                out=biased[:],
                in0=out_bank_of[c][:],
                in1=b2_rows[:].unsqueeze(1).to_broadcast([P, SUBTILES, D_HET]),
                op=ALU.add,
            )
            biased_of[c] = biased

        def message(c):
            b = c // CHUNKS_PER_BLOCK
            if c % CHUNKS_PER_BLOCK == 0:
                msg_blk = block_pool.tile([P, EDGES_PER_PARTITION, D_HET], F32)
                msg_blocks[b] = msg_blk
            nc.vector.tensor_tensor(
                out=msg_blocks[b][:, own_edges(c), :],
                in0=biased_of[c][:],
                in1=f_blocks[b][:, own_edges(c), :],
                op=ALU.mult,
            )

        def sum_squares(c):
            b = c // CHUNKS_PER_BLOCK
            if c % CHUNKS_PER_BLOCK == 0:
                ss_blk = block_pool.tile([P, EDGES_PER_PARTITION], F32)
                ss_blocks[b] = ss_blk
            first = (c % CHUNKS_PER_BLOCK) * SUBTILES
            squares = work.tile([P, SUBTILES, D_HET], BF16)
            for a in range(SUBTILES):
                nc.scalar.activation(
                    out=squares[:, a, :],
                    in_=msg_blocks[b][:, first + a, :],
                    func=ACT.Square,
                    accum_out=ss_blocks[b][:, first + a : first + a + 1],
                )

        def clamp_sum(b):
            clamped = block_pool.tile([P, EDGES_PER_PARTITION], F32)
            nc.vector.tensor_scalar_max(out=clamped[:], in0=ss_blocks[b][:], scalar1=1.0)
            clamped_of[b] = clamped

        def root(b):
            norm = block_pool.tile([P, EDGES_PER_PARTITION], F32)
            nc.scalar.sqrt(out=norm[:], in_=clamped_of[b][:])
            norm_of[b] = norm

        def invert(b):
            factor = block_pool.tile([P, EDGES_PER_PARTITION], F32)
            nc.vector.reciprocal(out=factor[:], in_=norm_of[b][:])
            factor_of[b] = factor

        def scale_and_store(c):
            b = c // CHUNKS_PER_BLOCK
            result = work.tile([P, SUBTILES, D_HET], F32, bufs=3)
            if c < N_CHUNKS - TAIL_CHUNKS and c % SCALAR_SCALES_EVERY != SCALAR_SCALES_EVERY - 1:
                nc.vector.tensor_tensor(
                    out=result[:],
                    in0=msg_blocks[b][:, own_edges(c), :],
                    in1=factor_of[b][:, own_edges(c)].unsqueeze(2).to_broadcast([P, SUBTILES, D_HET]),
                    op=ALU.mult,
                )
            else:
                first = (c % CHUNKS_PER_BLOCK) * SUBTILES
                for a in range(SUBTILES):
                    nc.scalar.activation(
                        out=result[:, a, :],
                        in_=msg_blocks[b][:, first + a, :],
                        func=ACT.Copy,
                        scale=factor_of[b][:, first + a : first + a + 1],
                    )
            nc.sync.dma_start(out=block_rows(out, b)[:, own_edges(c), :], in_=result[:])

        def chunk(c):
            return 0 <= c < N_CHUNKS

        transpose_mij(0)
        for w in range(N_CHUNKS + 7):
            new_factors = chunk(w - 5) and (w - 5) % CHUNKS_PER_BLOCK == 0
            if new_factors:
                clamp_sum((w - 5) // CHUNKS_PER_BLOCK)
            if chunk(w):
                gather_mij(w)
            if new_factors:
                root((w - 5) // CHUNKS_PER_BLOCK)
            if chunk(w + 1):
                transpose_mij(w + 1)
            if chunk(w + 3):
                load_chunk(w + 3)
            if chunk(w - 2):
                regroup_h(w - 2)
            if chunk(w - 3):
                add_b2(w - 3)
            if chunk(w - 1):
                bias_relu(w - 1)
            if chunk(w):
                quantise_mij(w)
                layer1(w)
            if chunk(w - 3):
                message(w - 3)
            if chunk(w - 2):
                quantise_h(w - 2)
                layer2(w - 2)
            if chunk(w - 3):
                sum_squares(w - 3)
            if chunk(w - 6):
                scale_and_store(w - 6)
            if new_factors:
                invert((w - 5) // CHUNKS_PER_BLOCK)
